import numpy as np
import ml_dtypes


def mxq(x, axis, fmt="e4m3"):
    dtype, down = {"e4m3": (ml_dtypes.float8_e4m3fn, 7), "e5m2": (ml_dtypes.float8_e5m2, 14)}[fmt]
    v = np.moveaxis(np.asarray(x, np.float32).astype(ml_dtypes.bfloat16).astype(np.float64), axis, -1)
    blocks = v.reshape(v.shape[:-1] + (-1, 32))
    amax = np.abs(blocks).max(-1, keepdims=True)
    byte = np.maximum(np.where(amax > 0, np.frexp(amax)[1] - 1 + 127, 0) - down, 1)
    scale = np.exp2(byte - 127.0)
    codes = (blocks / scale).astype(np.float32).astype(dtype).astype(np.float64)
    return np.moveaxis((codes * scale).reshape(v.shape), -1, axis)


WIDE = False


def mx_kscale(k):
    if not WIDE:
        return np.ones(k)
    levels = np.array([10, -10, 5, -5, 0])
    if k % 512:
        return np.exp2(np.random.permutation(np.resize(levels, k // 32))).repeat(32)
    a = np.empty((k // 512, 16))
    for p in range(k // 512):
        a[p, :8] = np.random.permutation(np.resize(levels, 8))
        for g in range(8):
            far = levels[np.abs(levels - a[p, g]) >= 10]
            a[p, g + 8] = far[np.random.randint(len(far))]
    return np.exp2(a.ravel()).repeat(32)


BF16 = ml_dtypes.bfloat16


def bf(x):
    return np.asarray(x, np.float32).astype(BF16)


def f64(x):
    return np.asarray(x).astype(np.float64)


B, SIDE, HE, Z, HD, XO = 4096, 32, 1024, 512, 256, 1024


def setup_inputs():
    n = np.random.standard_normal
    s, t = mx_kscale(HE), mx_kscale(Z)
    return {"h": bf(np.tanh(n((B, HE))) * s),
            "W_mu_e": bf(n((Z, HE)) * 1.5 / np.sqrt(HE) / s[None, :] * t[:, None]),
            "b_mu_e": bf(n(Z) * 0.3 * t),
            "W_ls_e": bf(n((Z, HE)) * 1.5 / np.sqrt(HE) / s[None, :]),
            "b_ls_e": bf(n(Z) * 0.3),
            "eps_z": bf(n((B, Z)) * t),
            "W_in_d": bf(n((HD, Z)) * 0.6 / np.sqrt(Z) / t[None, :]),
            "b_in_d": bf(n(HD) * 0.3)}


def reference(h, W_mu_e, b_mu_e, W_ls_e, b_ls_e, eps_z, W_in_d, b_in_d):
    hq = mxq(f64(h), 1, "e4m3")
    mu_e = (hq @ mxq(f64(W_mu_e), 1, "e4m3").T) + f64(b_mu_e)
    ls_e = (hq @ mxq(f64(W_ls_e), 1, "e4m3").T) + f64(b_ls_e)
    z = mu_e + np.exp(0.5 * ls_e) * f64(eps_z)
    return np.tanh((mxq(z, 1, "e4m3") @ mxq(f64(W_in_d), 1, "e4m3").T) + f64(b_in_d))

@@ -1,0 +1,431 @@
+from contextlib import ExitStack
+
+import concourse.mybir as mybir
+from concourse.masks import make_identity
+
+F32 = mybir.dt.float32
+BF16 = mybir.dt.bfloat16
+U32 = mybir.dt.uint32
+U8 = mybir.dt.uint8
+FP8X4 = mybir.dt.float8_e4m3fn_x4
+AF = mybir.ActivationFunctionType
+ALU = mybir.AluOpType
+
+P = 128
+B, HE, Z, HD = 4096, 1024, 512, 256
+FLOPS = 2 * B * HE * 2 * Z + 2 * B * Z * HD
+
+CHUNK_TILES = [4, 4, 4, 4, 4, 4, 4, 4]
+MANUAL = True
+REGROUP = "pool"
+POOL_ADD_EVERY = 0
+
+
+def tile_vae_pa_t_kernel(
+    tc, h, W_mu_e, b_mu_e, W_ls_e, b_ls_e, eps_z, W_in_d, b_in_d, out
+):
+    nc = tc.nc
+    n_chunks = len(CHUNK_TILES)
+    row0 = [P * sum(CHUNK_TILES[:c]) for c in range(n_chunks)]
+    width = [P * nb for nb in CHUNK_TILES]
+
+    with ExitStack() as ctx:
+        const = ctx.enter_context(tc.tile_pool(name="const", bufs=1))
+        gpool = ctx.enter_context(tc.tile_pool(name="gpool", bufs=4))
+        wpool = ctx.enter_context(tc.tile_pool(name="wpool", bufs=6))
+        spool = ctx.enter_context(tc.tile_pool(name="spool", bufs=4))
+        zpool = ctx.enter_context(tc.tile_pool(name="zpool", bufs=2))
+        zwpool = ctx.enter_context(tc.tile_pool(name="zwpool", bufs=3))
+        opool = ctx.enter_context(tc.tile_pool(name="opool", bufs=8))
+        ps_xy = ctx.enter_context(tc.psum_pool(name="ps_xy", bufs=2))
+        ps_e = ctx.enter_context(tc.psum_pool(name="ps_e", bufs=1))
+        ps_o = ctx.enter_context(tc.psum_pool(name="ps_o", bufs=1))
+        ps_mm = ctx.enter_context(tc.psum_pool(name="ps_mm", bufs=4))
+        if MANUAL:
+            ctx.enter_context(tc.manual_schedule())
+
+        w_src = {"ls": W_ls_e, "mu": W_mu_e}
+        w_raw = {}
+        for u in range(2):
+            for which in ("ls", "mu"):
+                nm = "wraw_%s%d" % (which, u)
+                w_raw[(which, u)] = const.tile([P, 2 * HE], BF16, name=nm, tag=nm)
+        win_raw = const.tile([P, 2 * Z], BF16, name="win_raw", tag="win_raw")
+        h_sb = [
+            const.tile([P, CHUNK_TILES[c] * HE], BF16, name="h_sb%d" % c, tag="h_sb%d" % c)
+            for c in range(n_chunks)
+        ]
+        e_sb = [
+            const.tile([P, CHUNK_TILES[c] * Z], BF16, name="e_sb%d" % c, tag="e_sb%d" % c)
+            for c in range(n_chunks)
+        ]
+
+        def load_w(which, u):
+            nc.sync.dma_start(
+                out=w_raw[(which, u)][:],
+                in_=w_src[which].rearrange("(p u e) k -> p u (e k)", u=2, e=2)[:, u, :],
+            )
+
+        def load_h(c):
+            nc.sync.dma_start(
+                out=h_sb[c][:],
+                in_=h[row0[c] : row0[c] + width[c], :].rearrange(
+                    "(p i) k -> p (i k)", i=CHUNK_TILES[c]
+                ),
+            )
+
+        def load_e(c):
+            nc.sync.dma_start(
+                out=e_sb[c][:],
+                in_=eps_z[row0[c] : row0[c] + width[c], :].rearrange(
+                    "(p i) k -> p (i k)", i=CHUNK_TILES[c]
+                ),
+            )
+
+        bmu_raw = const.tile([P, 4], BF16, name="bmu_raw", tag="bmu_raw")
+        bls_raw = const.tile([P, 4], BF16, name="bls_raw", tag="bls_raw")
+        bin_row = const.tile([P, HD], BF16, name="bin_row", tag="bin_row")
+        ones = const.tile([P, P], BF16, name="ones", tag="ones")
+        warm = const.tile([P, 1], F32, name="warm", tag="warm")
+        warm2 = const.tile([P, 1], F32, name="warm2", tag="warm2")
+        nc.vector.memset(warm[:], 0.0)
+        nc.vector.memset(bin_row[:], 0.0)
+        nc.vector.memset(ones[:], 1.0)
+        nc.scalar.dma_start(out=bin_row[0:1, :], in_=b_in_d.rearrange("(o n) -> o n", o=1))
+        nc.scalar.dma_start(out=bls_raw[:], in_=b_ls_e.rearrange("(p t) -> p t", t=4))
+        nc.scalar.dma_start(out=bmu_raw[:], in_=b_mu_e.rearrange("(p t) -> p t", t=4))
+        nc.scalar.activation(out=warm2[:], in_=warm[:], func=AF.Exp)
+
+        load_w("ls", 0)
+        load_h(0)
+        load_w("mu", 0)
+        load_w("ls", 1)
+        load_w("mu", 1)
+        load_e(0)
+        load_h(1)
+        load_e(1)
+        nc.sync.dma_start(
+            out=win_raw[:].rearrange("p (j k) -> p j k", j=2),
+            in_=W_in_d.rearrange("(j p) k -> p j k", j=2),
+        )
+        for c in range(2, n_chunks):
+            load_h(c)
+            load_e(c)
+
+        ident = const.tile([P, P], F32, name="ident", tag="ident")
+        make_identity(nc, ident[:])
+
+        def transpose_pairs(bank, src32, groups, stride, off):
+            view = bank[:].rearrange("p (v n) -> p v n", v=2)
+            for j, i in enumerate(groups):
+                for v in range(2):
+                    w0 = i * stride + off + v
+                    nc.tensor.transpose(
+                        out=view[:, v, j * P : (j + 1) * P],
+                        in_=src32[:, w0 : w0 + 2 * P - 1 : 2],
+                        identity=ident[:],
+                    )
+
+        def copy_out(engine, bank, dst32):
+            src = bank[:].rearrange("p (v n) -> p n v", v=2)
+            dst = dst32.rearrange("p (n v) -> p n v", v=2)
+            if engine == "act":
+                nc.scalar.copy(out=dst, in_=src)
+            else:
+                nc.vector.tensor_copy(out=dst, in_=src)
+
+        def quantise(grp, cols, words, scales):
+            nc.vector.quantize_mx(
+                out=words[:, :cols].bitcast(FP8X4), scales=scales[:, :cols], in_=grp[:, : 4 * cols]
+            )
+
+        def bank_of(pool):
+            if pool == "xy":
+                return ps_xy.tile([P, 512], F32, name="xy", tag="xy")
+            if pool == "o":
+                return ps_o.tile([P, 512], F32, name="o_bank", tag="o_bank")
+            return ps_mm.tile([P, 512], F32, name="acc", tag="acc")
+
+        def new_grp():
+            return gpool.tile([P, 2048], BF16, name="grp", tag="grp", align_bytes=64)
+
+        h32 = [t[:].bitcast(F32) for t in h_sb]
+        e32 = [t[:].bitcast(F32) for t in e_sb]
+        hw = {}
+        hs = {}
+        ww = {}
+        ws = {}
+
+        def tr_w(which, u, pool):
+            raw32 = w_raw[(which, u)][:].bitcast(F32)
+            banks = []
+            for g in range(2):
+                bank = bank_of(pool)
+                transpose_pairs(bank, raw32, [0, 1], 512, g * 256)
+                banks.append(bank)
+            return banks
+
+        def tr_h(c, g, pool):
+            banks = []
+            for b2 in range(CHUNK_TILES[c] // 2):
+                bank = bank_of(pool)
+                transpose_pairs(bank, h32[c], [2 * b2, 2 * b2 + 1], 512, g * 256)
+                banks.append(bank)
+            return banks
+
+        def copy_banks(banks, engines):
+            grp = new_grp()
+            g32 = grp[:].bitcast(F32)
+            for k, bank in enumerate(banks):
+                copy_out(engines[k % len(engines)], bank, g32[:, k * 512 : (k + 1) * 512])
+            return grp
+
+        def q_w(which, u, grp):
+            nm = "%s%d" % (which, u)
+            ww[(which, u)] = const.tile([P, 512], U32, name="ww" + nm, tag="ww" + nm, align_bytes=64)
+            ws[(which, u)] = const.tile([P, 512], U8, name="ws" + nm, tag="ws" + nm, align_bytes=64)
+            quantise(grp, 512, ww[(which, u)], ws[(which, u)])
+
+        def q_h(c, g, grp):
+            hw[(c, g)] = wpool.tile([P, 512], U32, name="hw", tag="hw", align_bytes=64)
+            hs[(c, g)] = wpool.tile([P, 512], U8, name="hs", tag="hs", align_bytes=64)
+            quantise(grp, width[c], hw[(c, g)], hs[(c, g)])
+
+        def tr_e(c, u):
+            e_bank = ps_e.tile([P, 512], F32, name="e_bank", tag="e_bank")
+            for i in range(CHUNK_TILES[c]):
+                w0 = i * 256 + u
+                nc.tensor.transpose(
+                    out=e_bank[:, i * P : (i + 1) * P], in_=e32[c][:, w0 : w0 + 2 * P - 1 : 2], identity=ident[:]
+                )
+            return e_bank
+
+        def mx1(which, c, u, e):
+            n = width[c]
+            acc = bank_of("mm")
+            for g in range(2):
+                col = g * 256 + e * P
+                nc.tensor.matmul_mx(
+                    out=acc[:, :n],
+                    lhsT=ww[(which, u)][:, col : col + P].bitcast(FP8X4),
+                    lhsT_scale=ws[(which, u)][:, col : col + P],
+                    rhs=hw[(c, g)][:, :n].bitcast(FP8X4),
+                    rhs_scale=hs[(c, g)][:, :n],
+                    start=(g == 0),
+                    stop=(g == 1),
+                )
+            return acc
+
+        def do_exp(c, u, ls):
+            n = width[c]
+            s_t = []
+            for e in range(2):
+                t = 2 * u + e
+                s = spool.tile([P, 512], F32, name="s", tag="s")
+                nc.scalar.activation(
+                    out=s[:, :n], in_=ls[e][:, :n], func=AF.Exp, bias=blsh[:, t : t + 1], scale=0.5
+                )
+                s_t.append(s)
+            return s_t
+
+        def do_a(c, u, e_bank, s_t):
+            n = width[c]
+            e_view = e_bank[:, :n].bitcast(BF16).rearrange("p (n e) -> p e n", e=2)
+            tts = []
+            for e in range(2):
+                tt = spool.tile([P, 512], F32, name="tt", tag="tt")
+                nc.vector.tensor_tensor(
+                    out=tt[:, :n], in0=e_view[:, e, :], in1=s_t[e][:, :n], op=ALU.mult
+                )
+                tts.append(tt)
+            return tts
+
+        zp = {}
+        zg = {}
+        zw = {}
+        zs = {}
+
+        def do_b(c, u, mu, tt):
+            n = width[c]
+            if u == 0:
+                zp[c] = zpool.tile([P, 4, 512], BF16, name="zp", tag="zp")
+            for e in range(2):
+                t = 2 * u + e
+                nc.vector.scalar_tensor_tensor(
+                    out=zp[c][:, t, :n],
+                    in0=mu[e][:, :n],
+                    scalar=bmu[:, t : t + 1],
+                    in1=tt[e][:, :n],
+                    op0=ALU.add,
+                    op1=ALU.add,
+                )
+
+        def regroup(c, engine):
+            n = width[c]
+            zg[c] = zpool.tile([P, 2048], BF16, name="zg", tag="zg", align_bytes=64)
+            if engine == "pool":
+                nc.gpsimd.tensor_scalar(
+                    out=zg[c][:, : 4 * n].rearrange("p (n t) -> p n t", t=4),
+                    in0=zp[c][:, :, :n].rearrange("p t n -> p n t"),
+                    scalar1=1.0,
+                    scalar2=0.0,
+                    op0=ALU.mult,
+                    op1=ALU.add,
+                )
+            else:
+                nc.vector.tensor_copy(
+                    out=zg[c][:, : 4 * n].rearrange("p (c i t) -> p c t i", i=4, t=4),
+                    in_=zp[c][:, :, :n].rearrange("p t (c i) -> p c t i", i=4),
+                )
+
+        def q_z(c):
+            zw[c] = zwpool.tile([P, 512], U32, name="zw", tag="zw", align_bytes=64)
+            zs[c] = zwpool.tile([P, 512], U8, name="zs", tag="zs", align_bytes=64)
+            quantise(zg[c], width[c], zw[c], zs[c])
+
+        def do_s(c, unit, pool):
+            o = bank_of(pool)
+            for j in range(2):
+                i = 2 * unit + j
+                nc.tensor.matmul_mx(
+                    out=o[:, j * HD : (j + 1) * HD],
+                    lhsT=zw[c][:, i * P : (i + 1) * P].bitcast(FP8X4),
+                    lhsT_scale=zs[c][:, i * P : (i + 1) * P],
+                    rhs=winw[:].bitcast(FP8X4),
+                    rhs_scale=wins[:],
+                    start=True,
+                    stop=True,
+                )
+            return (c, unit, o)
+
+        def do_add(item):
+            c, unit, o = item
+            o_sb = opool.tile([P, 512], F32, name="o_sb", tag="o_sb")
+            nc.vector.tensor_tensor(out=o_sb[:], in0=o[:], in1=bin_bc[:], op=ALU.add)
+            return (c, unit, o_sb)
+
+        def do_add_pool(item):
+            c, unit, o = item
+            o_sb = opool.tile([P, 512], F32, name="o_sb", tag="o_sb")
+            nc.scalar.copy(out=o_sb[:], in_=o[:])
+            nc.gpsimd.tensor_tensor(out=o_sb[:], in0=o_sb[:], in1=bin_bc[:], op=ALU.add)
+            return (c, unit, o_sb)
+
+        def do_tanh_store(item):
+            c, unit, o_sb = item
+            nc.scalar.activation(out=o_sb[:], in_=o_sb[:], func=AF.Tanh)
+            view = out[row0[c] : row0[c] + width[c], :].rearrange(
+                "(p i) d -> p (i d)", i=CHUNK_TILES[c]
+            )
+            nc.sync.dma_start(out=view[:, unit * 512 : (unit + 1) * 512], in_=o_sb[:])
+
+        bmu = const.tile([P, 4], F32, name="bmu", tag="bmu")
+        blsh = const.tile([P, 4], F32, name="blsh", tag="blsh")
+        bin_bc = const.tile([P, 2 * HD], F32, name="bin_bc", tag="bin_bc")
+        winw = const.tile([P, HD], U32, name="winw", tag="winw", align_bytes=64)
+        wins = const.tile([P, HD], U8, name="wins", tag="wins", align_bytes=64)
+
+        g_ls0 = copy_banks(tr_w("ls", 0, "mm"), ["act"])
+        g_h00 = copy_banks(tr_h(0, 0, "xy"), ["act", "dve"])
+        q_w("ls", 0, g_ls0)
+        g_h01 = copy_banks(tr_h(0, 1, "mm"), ["act", "dve"])
+        q_h(0, 0, g_h00)
+        g_mu0 = copy_banks(tr_w("mu", 0, "xy"), ["act"])
+        q_h(0, 1, g_h01)
+        nc.vector.tensor_copy(out=bmu[:], in_=bmu_raw[:])
+        nc.vector.tensor_scalar_mul(out=blsh[:], in0=bls_raw[:], scalar1=0.5)
+        g_ls1 = copy_banks(tr_w("ls", 1, "mm"), ["act"])
+        q_w("mu", 0, g_mu0)
+        banks_mu1 = tr_w("mu", 1, "xy")
+        ls = [mx1("ls", 0, 0, e) for e in range(2)]
+        s_t = do_exp(0, 0, ls)
+        g_mu1 = copy_banks(banks_mu1, ["act"])
+        q_w("ls", 1, g_ls1)
+        e_bank = tr_e(0, 0)
+        mu = [mx1("mu", 0, 0, e) for e in range(2)]
+        tts = do_a(0, 0, e_bank, s_t)
+        banks10 = tr_h(1, 0, "xy")
+        ls = [mx1("ls", 0, 1, e) for e in range(2)]
+        q_w("mu", 1, g_mu1)
+        g_h10 = copy_banks(banks10, ["act"])
+        do_b(0, 0, mu, tts)
+        s_t = do_exp(0, 1, ls)
+        e_bank = tr_e(0, 1)
+        banks11 = tr_h(1, 1, "xy")
+        mu = [mx1("mu", 0, 1, e) for e in range(2)]
+        g_h11 = copy_banks(banks11, ["act"])
+        q_h(1, 0, g_h10)
+        tts = do_a(0, 1, e_bank, s_t)
+        q_h(1, 1, g_h11)
+        pend_b = (0, 1, mu, tts)
+
+        pend_add = []
+        added_late = []
+        s_fifo = []
+        s_head = 0
+        for c in range(1, n_chunks):
+            nxt = c + 1 < n_chunks
+            grp = [None, None]
+            for u in range(2):
+                banks = tr_h(c + 1, u, "xy") if nxt else []
+                e_bank = tr_e(c, u)
+                first = c == 1 and u == 0
+                if first:
+                    win_bank = bank_of("o")
+                    transpose_pairs(win_bank, win_raw[:].bitcast(F32), [0, 1], 256, 0)
+                do_b(*pend_b)
+                if nxt:
+                    grp[u] = copy_banks(banks, ["act"])
+                if first:
+                    g_win = copy_banks([win_bank], ["act"])
+                if u == 0:
+                    regroup(c - 1, REGROUP)
+                added = added_late + [do_add(item) for item in pend_add]
+                pend_add = []
+                added_late = []
+                if u == 1:
+                    if c == 1:
+                        quantise(g_win, HD, winw, wins)
+                    q_z(c - 1)
+                    s_fifo.extend([(c - 1, unit) for unit in range(CHUNK_TILES[c - 1] // 2)])
+                    if nxt:
+                        q_h(c + 1, 0, grp[0])
+                ls = [mx1("ls", c, u, e) for e in range(2)]
+                mu = [mx1("mu", c, u, e) for e in range(2)]
+                if first:
+                    bin_bank = bank_of("o")
+                    nc.tensor.matmul(
+                        out=bin_bank[:, :HD], lhsT=ones[:], rhs=bin_row[:], start=True, stop=True
+                    )
+                o_item = None
+                if s_head < len(s_fifo):
+                    o_item = do_s(s_fifo[s_head][0], s_fifo[s_head][1], "o")
+                    s_head += 1
+                s_t = do_exp(c, u, ls)
+                if first:
+                    nc.scalar.copy(out=bin_bc[:, :HD], in_=bin_bank[:, :HD])
+                    nc.scalar.copy(out=bin_bc[:, HD:], in_=bin_bank[:, :HD])
+                if o_item is not None:
+                    if POOL_ADD_EVERY > 0 and s_head % POOL_ADD_EVERY == 0:
+                        added_late.append(do_add_pool(o_item))
+                    else:
+                        pend_add.append(o_item)
+                for item in added:
+                    do_tanh_store(item)
+                tts = do_a(c, u, e_bank, s_t)
+                if u == 1 and nxt:
+                    q_h(c + 1, 1, grp[1])
+                pend_b = (c, u, mu, tts)
+
+        last = n_chunks - 1
+        do_b(*pend_b)
+        for sc, su in s_fifo[s_head:]:
+            pend_add.append(do_s(sc, su, "mm"))
+        regroup(last, "dve")
+        q_z(last)
+        added = added_late + [do_add(item) for item in pend_add]
+        for item in added:
+            do_tanh_store(item)
+        items = [do_s(last, unit, "mm") for unit in range(CHUNK_TILES[last] // 2)]
+        for item in items:
+            do_tanh_store(do_add(item))

@@ -34,6 +34,7 @@ def tile_vae_pa_t_kernel(
         gpool = ctx.enter_context(tc.tile_pool(name="gpool", bufs=4))
         wpool = ctx.enter_context(tc.tile_pool(name="wpool", bufs=6))
         spool = ctx.enter_context(tc.tile_pool(name="spool", bufs=4))
+        hppool = ctx.enter_context(tc.tile_pool(name="hppool", bufs=4))
         zpool = ctx.enter_context(tc.tile_pool(name="zpool", bufs=2))
         zwpool = ctx.enter_context(tc.tile_pool(name="zwpool", bufs=3))
         opool = ctx.enter_context(tc.tile_pool(name="opool", bufs=8))
@@ -115,15 +116,18 @@ def tile_vae_pa_t_kernel(
         ident = const.tile([P, P], F32, name="ident", tag="ident")
         make_identity(nc, ident[:])
 
-        def transpose_pairs(bank, src32, groups, stride, off):
+        def transpose_pairs(bank, src32, groups, stride, off, sorted_words=False):
             view = bank[:].rearrange("p (v n) -> p v n", v=2)
             for j, i in enumerate(groups):
                 for v in range(2):
-                    w0 = i * stride + off + v
+                    if sorted_words:
+                        w0 = i * stride + off + v * P
+                        words = src32[:, w0 : w0 + P]
+                    else:
+                        w0 = i * stride + off + v
+                        words = src32[:, w0 : w0 + 2 * P - 1 : 2]
                     nc.tensor.transpose(
-                        out=view[:, v, j * P : (j + 1) * P],
-                        in_=src32[:, w0 : w0 + 2 * P - 1 : 2],
-                        identity=ident[:],
+                        out=view[:, v, j * P : (j + 1) * P], in_=words, identity=ident[:]
                     )
 
         def copy_out(engine, bank, dst32):
@@ -153,6 +157,16 @@ def tile_vae_pa_t_kernel(
         e32 = [t[:].bitcast(F32) for t in e_sb]
         hw = {}
         hs = {}
+        hp = {}
+
+        def sort_words(c, g):
+            n_i = CHUNK_TILES[c]
+            hp[(c, g)] = hppool.tile([P, n_i * 256], F32, name="hp", tag="hp")
+            nc.scalar.copy(
+                out=hp[(c, g)][:].rearrange("p (i v w) -> p i v w", i=n_i, v=2),
+                in_=h32[c]
+                .rearrange("p (i g w v) -> p g i v w", i=n_i, g=2, v=2)[:, g, :, :, :],
+            )
         ww = {}
         ws = {}
 
@@ -169,7 +183,11 @@ def tile_vae_pa_t_kernel(
             banks = []
             for b2 in range(CHUNK_TILES[c] // 2):
                 bank = bank_of(pool)
-                transpose_pairs(bank, h32[c], [2 * b2, 2 * b2 + 1], 512, g * 256)
+                pair = [2 * b2, 2 * b2 + 1]
+                if (c, g) in hp:
+                    transpose_pairs(bank, hp[(c, g)][:], pair, 256, 0, sorted_words=True)
+                else:
+                    transpose_pairs(bank, h32[c], pair, 512, g * 256)
                 banks.append(bank)
             return banks
 
@@ -358,6 +376,8 @@ def tile_vae_pa_t_kernel(
         tts = do_a(0, 1, e_bank, s_t)
         q_h(1, 1, g_h11)
         pend_b = (0, 1, mu, tts)
+        sort_words(2, 0)
+        sort_words(2, 1)
 
         pend_add = []
         added_late = []
@@ -412,6 +432,8 @@ def tile_vae_pa_t_kernel(
                         pend_add.append(o_item)
                 for item in added:
                     do_tanh_store(item)
+                if c + 2 < n_chunks:
+                    sort_words(c + 2, u)
                 tts = do_a(c, u, e_bank, s_t)
                 if u == 1 and nxt:
                     q_h(c + 1, 1, grp[1])

@@ -67,6 +67,20 @@ def tile_vae_pa_t_kernel(
                 in_=w_src[which].rearrange("(p u e) k -> p u (e k)", u=2, e=2)[:, u, :],
             )
 
+        def load_w_row(which, u, e):
+            nc.sync.dma_start(
+                out=w_raw[(which, u)][:, e * HE : (e + 1) * HE],
+                in_=w_src[which].rearrange("(p u e) k -> p u e k", u=2, e=2)[:, u, e, :],
+            )
+
+        def load_h_pair(c, b2):
+            nc.sync.dma_start(
+                out=h_sb[c][:, 2 * b2 * HE : 2 * (b2 + 1) * HE].rearrange("p (i k) -> p i k", i=2),
+                in_=h[row0[c] : row0[c] + width[c], :].rearrange(
+                    "(p i) k -> p i k", i=CHUNK_TILES[c]
+                )[:, 2 * b2 : 2 * (b2 + 1), :],
+            )
+
         def load_h(c):
             nc.sync.dma_start(
                 out=h_sb[c][:],
@@ -97,8 +111,10 @@ def tile_vae_pa_t_kernel(
         nc.scalar.dma_start(out=bmu_raw[:], in_=b_mu_e.rearrange("(p t) -> p t", t=4))
         nc.scalar.activation(out=warm2[:], in_=warm[:], func=AF.Exp)
 
-        load_w("ls", 0)
-        load_h(0)
+        load_w_row("ls", 0, 0)
+        load_w_row("ls", 0, 1)
+        load_h_pair(0, 0)
+        load_h_pair(0, 1)
         load_w("mu", 0)
         load_w("ls", 1)
         load_w("mu", 1)
@@ -116,7 +132,7 @@ def tile_vae_pa_t_kernel(
         ident = const.tile([P, P], F32, name="ident", tag="ident")
         make_identity(nc, ident[:])
 
-        def transpose_pairs(bank, src32, groups, stride, off, sorted_words=False):
+        def transpose_pairs(bank, src32, groups, stride, off, sorted_words=False, j0=0):
             view = bank[:].rearrange("p (v n) -> p v n", v=2)
             for j, i in enumerate(groups):
                 for v in range(2):
@@ -127,7 +143,7 @@ def tile_vae_pa_t_kernel(
                         w0 = i * stride + off + v
                         words = src32[:, w0 : w0 + 2 * P - 1 : 2]
                     nc.tensor.transpose(
-                        out=view[:, v, j * P : (j + 1) * P], in_=words, identity=ident[:]
+                        out=view[:, v, (j0 + j) * P : (j0 + j + 1) * P], in_=words, identity=ident[:]
                     )
 
         def copy_out(engine, bank, dst32):
@@ -172,11 +188,10 @@ def tile_vae_pa_t_kernel(
 
         def tr_w(which, u, pool):
             raw32 = w_raw[(which, u)][:].bitcast(F32)
-            banks = []
-            for g in range(2):
-                bank = bank_of(pool)
-                transpose_pairs(bank, raw32, [0, 1], 512, g * 256)
-                banks.append(bank)
+            banks = [bank_of(pool), bank_of(pool)]
+            for e in range(2):
+                for g in range(2):
+                    transpose_pairs(banks[g], raw32, [e], 512, g * 256, j0=e)
             return banks
 
         def tr_h(c, g, pool):
@@ -210,7 +225,10 @@ def tile_vae_pa_t_kernel(
             quantise(grp, width[c], hw[(c, g)], hs[(c, g)])
 
         def tr_e(c, u):
-            e_bank = ps_e.tile([P, 512], F32, name="e_bank", tag="e_bank")
+            if c == n_chunks - 1:
+                e_bank = bank_of("xy")
+            else:
+                e_bank = ps_e.tile([P, 512], F32, name="e_bank", tag="e_bank")
             for i in range(CHUNK_TILES[c]):
                 w0 = i * 256 + u
                 nc.tensor.transpose(
@@ -344,9 +362,14 @@ def tile_vae_pa_t_kernel(
         wins = const.tile([P, HD], U8, name="wins", tag="wins", align_bytes=64)
 
         g_ls0 = copy_banks(tr_w("ls", 0, "mm"), ["act"])
-        g_h00 = copy_banks(tr_h(0, 0, "xy"), ["act", "dve"])
+        h0_banks = [[None, None], [None, None]]
+        for b2 in range(2):
+            for g in range(2):
+                h0_banks[g][b2] = bank_of("xy" if g == 0 else "mm")
+                transpose_pairs(h0_banks[g][b2], h32[0], [2 * b2, 2 * b2 + 1], 512, g * 256)
+        g_h00 = copy_banks(h0_banks[0], ["act", "dve"])
         q_w("ls", 0, g_ls0)
-        g_h01 = copy_banks(tr_h(0, 1, "mm"), ["act", "dve"])
+        g_h01 = copy_banks(h0_banks[1], ["act", "dve"])
         q_h(0, 0, g_h00)
         g_mu0 = copy_banks(tr_w("mu", 0, "xy"), ["act"])
         q_h(0, 1, g_h01)
@@ -376,8 +399,6 @@ def tile_vae_pa_t_kernel(
         tts = do_a(0, 1, e_bank, s_t)
         q_h(1, 1, g_h11)
         pend_b = (0, 1, mu, tts)
-        sort_words(2, 0)
-        sort_words(2, 1)
 
         pend_add = []
         added_late = []
@@ -432,7 +453,7 @@ def tile_vae_pa_t_kernel(
                         pend_add.append(o_item)
                 for item in added:
                     do_tanh_store(item)
-                if c + 2 < n_chunks:
+                if u == 1 and c + 2 < n_chunks:
                     sort_words(c + 2, u)
                 tts = do_a(c, u, e_bank, s_t)
                 if u == 1 and nxt:
@@ -443,11 +464,28 @@ def tile_vae_pa_t_kernel(
         do_b(*pend_b)
         for sc, su in s_fifo[s_head:]:
             pend_add.append(do_s(sc, su, "mm"))
-        regroup(last, "dve")
-        q_z(last)
-        added = added_late + [do_add(item) for item in pend_add]
+        zg[last] = zpool.tile([P, 2048], BF16, name="zg", tag="zg", align_bytes=64)
+        zw[last] = zwpool.tile([P, 512], U32, name="zw", tag="zw", align_bytes=64)
+        zs[last] = zwpool.tile([P, 512], U8, name="zs", tag="zs", align_bytes=64)
+        nc.vector.tensor_copy(
+            out=zg[last][:, :1024].rearrange("p (c i t) -> p c t i", i=4, t=4),
+            in_=zp[last][:, :, :256].rearrange("p t (c i) -> p c t i", i=4),
+        )
+        nc.scalar.copy(
+            out=zg[last][:, 1024:].rearrange("p (c i t) -> p c t i", i=4, t=4),
+            in_=zp[last][:, :, 256:].rearrange("p t (c i) -> p c t i", i=4),
+        )
+        added = added_late + [do_add(item) for item in pend_add[:1]]
+        for unit in range(2):
+            cols = slice(unit * 256, (unit + 1) * 256)
+            nc.vector.quantize_mx(
+                out=zw[last][:, cols].bitcast(FP8X4),
+                scales=zs[last][:, cols],
+                in_=zg[last][:, unit * 1024 : (unit + 1) * 1024],
+            )
+        items = [do_s(last, unit, "mm") for unit in range(2)]
+        added += [do_add(item) for item in pend_add[1:]]
         for item in added:
             do_tanh_store(item)
-        items = [do_s(last, unit, "mm") for unit in range(CHUNK_TILES[last] // 2)]
         for item in items:
             do_tanh_store(do_add(item))

from contextlib import ExitStack

import concourse.mybir as mybir
from concourse.masks import make_identity

F32 = mybir.dt.float32
BF16 = mybir.dt.bfloat16
U32 = mybir.dt.uint32
U8 = mybir.dt.uint8
FP8X4 = mybir.dt.float8_e4m3fn_x4
AF = mybir.ActivationFunctionType
ALU = mybir.AluOpType

P = 128
B, HE, Z, HD = 4096, 1024, 512, 256
FLOPS = 2 * B * HE * 2 * Z + 2 * B * Z * HD

CHUNK_TILES = [4, 4, 4, 4, 4, 4, 4, 4]
MANUAL = True
REGROUP = "pool"
POOL_ADD_EVERY = 0


def tile_vae_pa_t_kernel(
    tc, h, W_mu_e, b_mu_e, W_ls_e, b_ls_e, eps_z, W_in_d, b_in_d, out
):
    nc = tc.nc
    n_chunks = len(CHUNK_TILES)
    row0 = [P * sum(CHUNK_TILES[:c]) for c in range(n_chunks)]
    width = [P * nb for nb in CHUNK_TILES]

    with ExitStack() as ctx:
        const = ctx.enter_context(tc.tile_pool(name="const", bufs=1))
        gpool = ctx.enter_context(tc.tile_pool(name="gpool", bufs=4))
        wpool = ctx.enter_context(tc.tile_pool(name="wpool", bufs=6))
        spool = ctx.enter_context(tc.tile_pool(name="spool", bufs=4))
        hppool = ctx.enter_context(tc.tile_pool(name="hppool", bufs=4))
        zpool = ctx.enter_context(tc.tile_pool(name="zpool", bufs=2))
        zwpool = ctx.enter_context(tc.tile_pool(name="zwpool", bufs=3))
        opool = ctx.enter_context(tc.tile_pool(name="opool", bufs=8))
        ps_xy = ctx.enter_context(tc.psum_pool(name="ps_xy", bufs=2))
        ps_e = ctx.enter_context(tc.psum_pool(name="ps_e", bufs=1))
        ps_o = ctx.enter_context(tc.psum_pool(name="ps_o", bufs=1))
        ps_mm = ctx.enter_context(tc.psum_pool(name="ps_mm", bufs=4))
        if MANUAL:
            ctx.enter_context(tc.manual_schedule())

        w_src = {"ls": W_ls_e, "mu": W_mu_e}
        w_raw = {}
        for u in range(2):
            for which in ("ls", "mu"):
                nm = "wraw_%s%d" % (which, u)
                w_raw[(which, u)] = const.tile([P, 2 * HE], BF16, name=nm, tag=nm)
        win_raw = const.tile([P, 2 * Z], BF16, name="win_raw", tag="win_raw")
        h_sb = [
            const.tile([P, CHUNK_TILES[c] * HE], BF16, name="h_sb%d" % c, tag="h_sb%d" % c)
            for c in range(n_chunks)
        ]
        e_sb = [
            const.tile([P, CHUNK_TILES[c] * Z], BF16, name="e_sb%d" % c, tag="e_sb%d" % c)
            for c in range(n_chunks)
        ]

        def load_w(which, u):
            nc.sync.dma_start(
                out=w_raw[(which, u)][:],
                in_=w_src[which].rearrange("(p u e) k -> p u (e k)", u=2, e=2)[:, u, :],
            )

        def load_w_row(which, u, e):
            nc.sync.dma_start(
                out=w_raw[(which, u)][:, e * HE : (e + 1) * HE],
                in_=w_src[which].rearrange("(p u e) k -> p u e k", u=2, e=2)[:, u, e, :],
            )

        def load_h_pair(c, b2):
            nc.sync.dma_start(
                out=h_sb[c][:, 2 * b2 * HE : 2 * (b2 + 1) * HE].rearrange("p (i k) -> p i k", i=2),
                in_=h[row0[c] : row0[c] + width[c], :].rearrange(
                    "(p i) k -> p i k", i=CHUNK_TILES[c]
                )[:, 2 * b2 : 2 * (b2 + 1), :],
            )

        def load_h(c):
            nc.sync.dma_start(
                out=h_sb[c][:],
                in_=h[row0[c] : row0[c] + width[c], :].rearrange(
                    "(p i) k -> p (i k)", i=CHUNK_TILES[c]
                ),
            )

        def load_e(c):
            nc.sync.dma_start(
                out=e_sb[c][:],
                in_=eps_z[row0[c] : row0[c] + width[c], :].rearrange(
                    "(p i) k -> p (i k)", i=CHUNK_TILES[c]
                ),
            )

        bmu_raw = const.tile([P, 4], BF16, name="bmu_raw", tag="bmu_raw")
        bls_raw = const.tile([P, 4], BF16, name="bls_raw", tag="bls_raw")
        bin_row = const.tile([P, HD], BF16, name="bin_row", tag="bin_row")
        ones = const.tile([P, P], BF16, name="ones", tag="ones")
        warm = const.tile([P, 1], F32, name="warm", tag="warm")
        warm2 = const.tile([P, 1], F32, name="warm2", tag="warm2")
        nc.vector.memset(warm[:], 0.0)
        nc.vector.memset(bin_row[:], 0.0)
        nc.vector.memset(ones[:], 1.0)
        nc.scalar.dma_start(out=bin_row[0:1, :], in_=b_in_d.rearrange("(o n) -> o n", o=1))
        nc.scalar.dma_start(out=bls_raw[:], in_=b_ls_e.rearrange("(p t) -> p t", t=4))
        nc.scalar.dma_start(out=bmu_raw[:], in_=b_mu_e.rearrange("(p t) -> p t", t=4))
        nc.scalar.activation(out=warm2[:], in_=warm[:], func=AF.Exp)

        load_w_row("ls", 0, 0)
        load_w_row("ls", 0, 1)
        load_h_pair(0, 0)
        load_h_pair(0, 1)
        load_w("mu", 0)
        load_w("ls", 1)
        load_w("mu", 1)
        load_e(0)
        load_h(1)
        load_e(1)
        nc.sync.dma_start(
            out=win_raw[:].rearrange("p (j k) -> p j k", j=2),
            in_=W_in_d.rearrange("(j p) k -> p j k", j=2),
        )
        for c in range(2, n_chunks):
            load_h(c)
            load_e(c)

        ident = const.tile([P, P], F32, name="ident", tag="ident")
        make_identity(nc, ident[:])

        def transpose_pairs(bank, src32, groups, stride, off, sorted_words=False, j0=0):
            view = bank[:].rearrange("p (v n) -> p v n", v=2)
            for j, i in enumerate(groups):
                for v in range(2):
                    if sorted_words:
                        w0 = i * stride + off + v * P
                        words = src32[:, w0 : w0 + P]
                    else:
                        w0 = i * stride + off + v
                        words = src32[:, w0 : w0 + 2 * P - 1 : 2]
                    nc.tensor.transpose(
                        out=view[:, v, (j0 + j) * P : (j0 + j + 1) * P], in_=words, identity=ident[:]
                    )

        def copy_out(engine, bank, dst32):
            src = bank[:].rearrange("p (v n) -> p n v", v=2)
            dst = dst32.rearrange("p (n v) -> p n v", v=2)
            if engine == "act":
                nc.scalar.copy(out=dst, in_=src)
            else:
                nc.vector.tensor_copy(out=dst, in_=src)

        def quantise(grp, cols, words, scales):
            nc.vector.quantize_mx(
                out=words[:, :cols].bitcast(FP8X4), scales=scales[:, :cols], in_=grp[:, : 4 * cols]
            )

        def bank_of(pool):
            if pool == "xy":
                return ps_xy.tile([P, 512], F32, name="xy", tag="xy")
            if pool == "o":
                return ps_o.tile([P, 512], F32, name="o_bank", tag="o_bank")
            return ps_mm.tile([P, 512], F32, name="acc", tag="acc")

        def new_grp():
            return gpool.tile([P, 2048], BF16, name="grp", tag="grp", align_bytes=64)

        h32 = [t[:].bitcast(F32) for t in h_sb]
        e32 = [t[:].bitcast(F32) for t in e_sb]
        hw = {}
        hs = {}
        hp = {}

        def sort_words(c, g):
            n_i = CHUNK_TILES[c]
            hp[(c, g)] = hppool.tile([P, n_i * 256], F32, name="hp", tag="hp")
            nc.scalar.copy(
                out=hp[(c, g)][:].rearrange("p (i v w) -> p i v w", i=n_i, v=2),
                in_=h32[c]
                .rearrange("p (i g w v) -> p g i v w", i=n_i, g=2, v=2)[:, g, :, :, :],
            )
        ww = {}
        ws = {}

        def tr_w(which, u, pool):
            raw32 = w_raw[(which, u)][:].bitcast(F32)
            banks = [bank_of(pool), bank_of(pool)]
            for e in range(2):
                for g in range(2):
                    transpose_pairs(banks[g], raw32, [e], 512, g * 256, j0=e)
            return banks

        def tr_h(c, g, pool):
            banks = []
            for b2 in range(CHUNK_TILES[c] // 2):
                bank = bank_of(pool)
                pair = [2 * b2, 2 * b2 + 1]
                if (c, g) in hp:
                    transpose_pairs(bank, hp[(c, g)][:], pair, 256, 0, sorted_words=True)
                else:
                    transpose_pairs(bank, h32[c], pair, 512, g * 256)
                banks.append(bank)
            return banks

        def copy_banks(banks, engines):
            grp = new_grp()
            g32 = grp[:].bitcast(F32)
            for k, bank in enumerate(banks):
                copy_out(engines[k % len(engines)], bank, g32[:, k * 512 : (k + 1) * 512])
            return grp

        def q_w(which, u, grp):
            nm = "%s%d" % (which, u)
            ww[(which, u)] = const.tile([P, 512], U32, name="ww" + nm, tag="ww" + nm, align_bytes=64)
            ws[(which, u)] = const.tile([P, 512], U8, name="ws" + nm, tag="ws" + nm, align_bytes=64)
            quantise(grp, 512, ww[(which, u)], ws[(which, u)])

        def q_h(c, g, grp):
            hw[(c, g)] = wpool.tile([P, 512], U32, name="hw", tag="hw", align_bytes=64)
            hs[(c, g)] = wpool.tile([P, 512], U8, name="hs", tag="hs", align_bytes=64)
            quantise(grp, width[c], hw[(c, g)], hs[(c, g)])

        def tr_e(c, u):
            if c == n_chunks - 1:
                e_bank = bank_of("xy")
            else:
                e_bank = ps_e.tile([P, 512], F32, name="e_bank", tag="e_bank")
            for i in range(CHUNK_TILES[c]):
                w0 = i * 256 + u
                nc.tensor.transpose(
                    out=e_bank[:, i * P : (i + 1) * P], in_=e32[c][:, w0 : w0 + 2 * P - 1 : 2], identity=ident[:]
                )
            return e_bank

        def mx1(which, c, u, e):
            n = width[c]
            acc = bank_of("mm")
            for g in range(2):
                col = g * 256 + e * P
                nc.tensor.matmul_mx(
                    out=acc[:, :n],
                    lhsT=ww[(which, u)][:, col : col + P].bitcast(FP8X4),
                    lhsT_scale=ws[(which, u)][:, col : col + P],
                    rhs=hw[(c, g)][:, :n].bitcast(FP8X4),
                    rhs_scale=hs[(c, g)][:, :n],
                    start=(g == 0),
                    stop=(g == 1),
                )
            return acc

        def do_exp(c, u, ls):
            n = width[c]
            s_t = []
            for e in range(2):
                t = 2 * u + e
                s = spool.tile([P, 512], F32, name="s", tag="s")
                nc.scalar.activation(
                    out=s[:, :n], in_=ls[e][:, :n], func=AF.Exp, bias=blsh[:, t : t + 1], scale=0.5
                )
                s_t.append(s)
            return s_t

        def do_a(c, u, e_bank, s_t):
            n = width[c]
            e_view = e_bank[:, :n].bitcast(BF16).rearrange("p (n e) -> p e n", e=2)
            tts = []
            for e in range(2):
                tt = spool.tile([P, 512], F32, name="tt", tag="tt")
                nc.vector.tensor_tensor(
                    out=tt[:, :n], in0=e_view[:, e, :], in1=s_t[e][:, :n], op=ALU.mult
                )
                tts.append(tt)
            return tts

        zp = {}
        zg = {}
        zw = {}
        zs = {}

        def do_b(c, u, mu, tt):
            n = width[c]
            if u == 0:
                zp[c] = zpool.tile([P, 4, 512], BF16, name="zp", tag="zp")
            for e in range(2):
                t = 2 * u + e
                nc.vector.scalar_tensor_tensor(
                    out=zp[c][:, t, :n],
                    in0=mu[e][:, :n],
                    scalar=bmu[:, t : t + 1],
                    in1=tt[e][:, :n],
                    op0=ALU.add,
                    op1=ALU.add,
                )

        def regroup(c, engine):
            n = width[c]
            zg[c] = zpool.tile([P, 2048], BF16, name="zg", tag="zg", align_bytes=64)
            if engine == "pool":
                nc.gpsimd.tensor_scalar(
                    out=zg[c][:, : 4 * n].rearrange("p (n t) -> p n t", t=4),
                    in0=zp[c][:, :, :n].rearrange("p t n -> p n t"),
                    scalar1=1.0,
                    scalar2=0.0,
                    op0=ALU.mult,
                    op1=ALU.add,
                )
            else:
                nc.vector.tensor_copy(
                    out=zg[c][:, : 4 * n].rearrange("p (c i t) -> p c t i", i=4, t=4),
                    in_=zp[c][:, :, :n].rearrange("p t (c i) -> p c t i", i=4),
                )

        def q_z(c):
            zw[c] = zwpool.tile([P, 512], U32, name="zw", tag="zw", align_bytes=64)
            zs[c] = zwpool.tile([P, 512], U8, name="zs", tag="zs", align_bytes=64)
            quantise(zg[c], width[c], zw[c], zs[c])

        def do_s(c, unit, pool):
            o = bank_of(pool)
            for j in range(2):
                i = 2 * unit + j
                nc.tensor.matmul_mx(
                    out=o[:, j * HD : (j + 1) * HD],
                    lhsT=zw[c][:, i * P : (i + 1) * P].bitcast(FP8X4),
                    lhsT_scale=zs[c][:, i * P : (i + 1) * P],
                    rhs=winw[:].bitcast(FP8X4),
                    rhs_scale=wins[:],
                    start=True,
                    stop=True,
                )
            return (c, unit, o)

        def do_add(item):
            c, unit, o = item
            o_sb = opool.tile([P, 512], F32, name="o_sb", tag="o_sb")
            nc.vector.tensor_tensor(out=o_sb[:], in0=o[:], in1=bin_bc[:], op=ALU.add)
            return (c, unit, o_sb)

        def do_add_pool(item):
            c, unit, o = item
            o_sb = opool.tile([P, 512], F32, name="o_sb", tag="o_sb")
            nc.scalar.copy(out=o_sb[:], in_=o[:])
            nc.gpsimd.tensor_tensor(out=o_sb[:], in0=o_sb[:], in1=bin_bc[:], op=ALU.add)
            return (c, unit, o_sb)

        def do_tanh_store(item):
            c, unit, o_sb = item
            nc.scalar.activation(out=o_sb[:], in_=o_sb[:], func=AF.Tanh)
            view = out[row0[c] : row0[c] + width[c], :].rearrange(
                "(p i) d -> p (i d)", i=CHUNK_TILES[c]
            )
            nc.sync.dma_start(out=view[:, unit * 512 : (unit + 1) * 512], in_=o_sb[:])

        bmu = const.tile([P, 4], F32, name="bmu", tag="bmu")
        blsh = const.tile([P, 4], F32, name="blsh", tag="blsh")
        bin_bc = const.tile([P, 2 * HD], F32, name="bin_bc", tag="bin_bc")
        winw = const.tile([P, HD], U32, name="winw", tag="winw", align_bytes=64)
        wins = const.tile([P, HD], U8, name="wins", tag="wins", align_bytes=64)

        g_ls0 = copy_banks(tr_w("ls", 0, "mm"), ["act"])
        h0_banks = [[None, None], [None, None]]
        for b2 in range(2):
            for g in range(2):
                h0_banks[g][b2] = bank_of("xy" if g == 0 else "mm")
                transpose_pairs(h0_banks[g][b2], h32[0], [2 * b2, 2 * b2 + 1], 512, g * 256)
        g_h00 = copy_banks(h0_banks[0], ["act", "dve"])
        q_w("ls", 0, g_ls0)
        g_h01 = copy_banks(h0_banks[1], ["act", "dve"])
        q_h(0, 0, g_h00)
        g_mu0 = copy_banks(tr_w("mu", 0, "xy"), ["act"])
        q_h(0, 1, g_h01)
        nc.vector.tensor_copy(out=bmu[:], in_=bmu_raw[:])
        nc.vector.tensor_scalar_mul(out=blsh[:], in0=bls_raw[:], scalar1=0.5)
        g_ls1 = copy_banks(tr_w("ls", 1, "mm"), ["act"])
        q_w("mu", 0, g_mu0)
        banks_mu1 = tr_w("mu", 1, "xy")
        ls = [mx1("ls", 0, 0, e) for e in range(2)]
        s_t = do_exp(0, 0, ls)
        g_mu1 = copy_banks(banks_mu1, ["act"])
        q_w("ls", 1, g_ls1)
        e_bank = tr_e(0, 0)
        mu = [mx1("mu", 0, 0, e) for e in range(2)]
        tts = do_a(0, 0, e_bank, s_t)
        banks10 = tr_h(1, 0, "xy")
        ls = [mx1("ls", 0, 1, e) for e in range(2)]
        q_w("mu", 1, g_mu1)
        g_h10 = copy_banks(banks10, ["act"])
        do_b(0, 0, mu, tts)
        s_t = do_exp(0, 1, ls)
        e_bank = tr_e(0, 1)
        banks11 = tr_h(1, 1, "xy")
        mu = [mx1("mu", 0, 1, e) for e in range(2)]
        g_h11 = copy_banks(banks11, ["act"])
        q_h(1, 0, g_h10)
        tts = do_a(0, 1, e_bank, s_t)
        q_h(1, 1, g_h11)
        pend_b = (0, 1, mu, tts)

        pend_add = []
        added_late = []
        s_fifo = []
        s_head = 0
        for c in range(1, n_chunks):
            nxt = c + 1 < n_chunks
            grp = [None, None]
            for u in range(2):
                banks = tr_h(c + 1, u, "xy") if nxt else []
                e_bank = tr_e(c, u)
                first = c == 1 and u == 0
                if first:
                    win_bank = bank_of("o")
                    transpose_pairs(win_bank, win_raw[:].bitcast(F32), [0, 1], 256, 0)
                do_b(*pend_b)
                if nxt:
                    grp[u] = copy_banks(banks, ["act"])
                if first:
                    g_win = copy_banks([win_bank], ["act"])
                if u == 0:
                    regroup(c - 1, REGROUP)
                added = added_late + [do_add(item) for item in pend_add]
                pend_add = []
                added_late = []
                if u == 1:
                    if c == 1:
                        quantise(g_win, HD, winw, wins)
                    q_z(c - 1)
                    s_fifo.extend([(c - 1, unit) for unit in range(CHUNK_TILES[c - 1] // 2)])
                    if nxt:
                        q_h(c + 1, 0, grp[0])
                ls = [mx1("ls", c, u, e) for e in range(2)]
                mu = [mx1("mu", c, u, e) for e in range(2)]
                if first:
                    bin_bank = bank_of("o")
                    nc.tensor.matmul(
                        out=bin_bank[:, :HD], lhsT=ones[:], rhs=bin_row[:], start=True, stop=True
                    )
                o_item = None
                if s_head < len(s_fifo):
                    o_item = do_s(s_fifo[s_head][0], s_fifo[s_head][1], "o")
                    s_head += 1
                s_t = do_exp(c, u, ls)
                if first:
                    nc.scalar.copy(out=bin_bc[:, :HD], in_=bin_bank[:, :HD])
                    nc.scalar.copy(out=bin_bc[:, HD:], in_=bin_bank[:, :HD])
                if o_item is not None:
                    if POOL_ADD_EVERY > 0 and s_head % POOL_ADD_EVERY == 0:
                        added_late.append(do_add_pool(o_item))
                    else:
                        pend_add.append(o_item)
                for item in added:
                    do_tanh_store(item)
                if u == 1 and c + 2 < n_chunks:
                    sort_words(c + 2, u)
                tts = do_a(c, u, e_bank, s_t)
                if u == 1 and nxt:
                    q_h(c + 1, 1, grp[1])
                pend_b = (c, u, mu, tts)

        last = n_chunks - 1
        do_b(*pend_b)
        for sc, su in s_fifo[s_head:]:
            pend_add.append(do_s(sc, su, "mm"))
        zg[last] = zpool.tile([P, 2048], BF16, name="zg", tag="zg", align_bytes=64)
        zw[last] = zwpool.tile([P, 512], U32, name="zw", tag="zw", align_bytes=64)
        zs[last] = zwpool.tile([P, 512], U8, name="zs", tag="zs", align_bytes=64)
        nc.vector.tensor_copy(
            out=zg[last][:, :1024].rearrange("p (c i t) -> p c t i", i=4, t=4),
            in_=zp[last][:, :, :256].rearrange("p t (c i) -> p c t i", i=4),
        )
        nc.scalar.copy(
            out=zg[last][:, 1024:].rearrange("p (c i t) -> p c t i", i=4, t=4),
            in_=zp[last][:, :, 256:].rearrange("p t (c i) -> p c t i", i=4),
        )
        added = added_late + [do_add(item) for item in pend_add[:1]]
        for unit in range(2):
            cols = slice(unit * 256, (unit + 1) * 256)
            nc.vector.quantize_mx(
                out=zw[last][:, cols].bitcast(FP8X4),
                scales=zs[last][:, cols],
                in_=zg[last][:, unit * 1024 : (unit + 1) * 1024],
            )
        items = [do_s(last, unit, "mm") for unit in range(2)]
        added += [do_add(item) for item in pend_add[1:]]
        for item in added:
            do_tanh_store(item)
        for item in items:
            do_tanh_store(do_add(item))
